import numpy as np
import ml_dtypes


def mxq(x, axis, fmt="e4m3"):
    dtype, down = {"e4m3": (ml_dtypes.float8_e4m3fn, 7), "e5m2": (ml_dtypes.float8_e5m2, 14)}[fmt]
    v = np.moveaxis(np.asarray(x, np.float32).astype(ml_dtypes.bfloat16).astype(np.float64), axis, -1)
    blocks = v.reshape(v.shape[:-1] + (-1, 32))
    amax = np.abs(blocks).max(-1, keepdims=True)
    byte = np.maximum(np.where(amax > 0, np.frexp(amax)[1] - 1 + 127, 0) - down, 1)
    scale = np.exp2(byte - 127.0)
    codes = (blocks / scale).astype(np.float32).astype(dtype).astype(np.float64)
    return np.moveaxis((codes * scale).reshape(v.shape), -1, axis)


WIDE = False


def mx_kscale(k):
    if not WIDE:
        return np.ones(k)
    levels = np.array([10, -10, 5, -5, 0])
    a = np.random.permutation(np.resize(levels, k // 512 * 4)).reshape(k // 512, 4)
    idx = np.arange(k)
    return np.exp2(a[idx // 512, idx % 128 // 32])


BF16 = ml_dtypes.bfloat16


def bf(x):
    return np.asarray(x, np.float32).astype(BF16)


def f64(x):
    return np.asarray(x).astype(np.float64)


E2M1 = np.array([0.0, 0.5, 1.0, 1.5, 2.0, 3.0, 4.0, 6.0, -0.0, -0.5, -1.0, -1.5, -2.0, -3.0, -4.0, -6.0])


def pack_weight(w, fmt):
    k, n = w.shape
    w = f64(bf(w)).reshape(k // 32, 32, n)
    amax = np.abs(w).max(1)
    if fmt == "e4m3":
        byte = np.frexp(amax)[1] - 1 + 127 - 7
    else:
        mant, ex = np.frexp(amax / 6.0)
        byte = np.where(mant > 0.5, ex, ex - 1) + 127
    byte = np.clip(np.where(amax > 0, byte, 1), 1, 254)
    scaled = (w * np.exp2(127.0 - byte)[:, None, :]).reshape(k, n).astype(np.float32)
    by_word = np.ascontiguousarray(scaled.reshape(k // 512, 128, 4, n).transpose(0, 1, 3, 2))
    if fmt == "e4m3":
        words = by_word.astype(ml_dtypes.float8_e4m3fn).view(np.uint8)
    else:
        c = by_word.astype(ml_dtypes.float4_e2m1fn).view(np.uint8) & 0xF
        words = c[..., 0::2] | (c[..., 1::2] << 4)
    return np.ascontiguousarray(words), np.ascontiguousarray(byte.astype(np.uint8).reshape(k // 512, 16, n))


def unpack_weight(words, scales, fmt):
    g, p, n, _ = words.shape
    if fmt == "e4m3":
        vals = np.ascontiguousarray(words).view(ml_dtypes.float8_e4m3fn).astype(np.float64)
    else:
        nib = np.empty((g, p, n, 4), np.uint8)
        nib[..., 0::2] = words & 0xF
        nib[..., 1::2] = words >> 4
        vals = E2M1[nib]
    vals = vals * np.repeat(np.exp2(scales.astype(np.float64) - 127.0), 8, axis=1)[..., None]
    return vals.transpose(0, 1, 3, 2).reshape(g * 512, n)


N, K, H = 2048, 8, 256


def sigmoid(v):
    return 1.0 / (1.0 + np.exp(-v))


def setup_inputs():
    s = mx_kscale(2 * H)[:H]
    s2 = np.concatenate([s, s])
    w = 1.0 / np.sqrt(H * (K + 2))
    mailbox_h = bf(np.random.standard_normal((N, K, H)) * s)
    mailbox_c = bf(np.random.standard_normal((N, K, H)) / np.sqrt(K))
    U_iou_w_words, U_iou_w_scales = pack_weight(np.ascontiguousarray((np.random.standard_normal((3 * H, 2 * H)) * w / s2).T), "e4m3")
    b_iou = bf(np.random.standard_normal((1, 3 * H)) * 0.1)
    U_f_w_words, U_f_w_scales = pack_weight(np.ascontiguousarray((np.random.standard_normal((H, 2 * H)) * w / s2).T), "e4m3")
    U_f_b = bf(np.random.standard_normal(H) * 0.1)
    return {"mailbox_h": mailbox_h,
            "mailbox_c": mailbox_c,
            "U_iou_w_words": U_iou_w_words,
            "U_iou_w_scales": U_iou_w_scales,
            "b_iou": b_iou,
            "U_f_w_words": U_f_w_words,
            "U_f_w_scales": U_f_w_scales,
            "U_f_b": U_f_b}


def reference(mailbox_h, mailbox_c, U_iou_w_words, U_iou_w_scales, b_iou, U_f_w_words, U_f_w_scales, U_f_b):
    mh = f64(mailbox_h)
    mc = f64(mailbox_c)
    h_cat = mh.sum(axis=1)
    h_max = mh.max(axis=1)
    h_combined = np.concatenate([h_cat, h_max], axis=1)
    hq = mxq(h_combined, 1, "e4m3")
    f = sigmoid((hq @ unpack_weight(U_f_w_words, U_f_w_scales, "e4m3")) + f64(U_f_b))
    c_agg = np.sum(f[:, None, :] * mc, axis=1)
    iou = hq @ unpack_weight(U_iou_w_words, U_iou_w_scales, "e4m3")
    iou = iou + f64(b_iou)
    i, o, u = np.split(iou, 3, axis=1)
    c = sigmoid(i) * np.tanh(u) + c_agg
    h = sigmoid(o) * np.tanh(c)
    return np.concatenate([h, c], axis=1)

@@ -1,0 +1,267 @@
+from contextlib import ExitStack
+
+import concourse.mybir as mybir
+from concourse.masks import make_identity
+
+F32 = mybir.dt.float32
+BF16 = mybir.dt.bfloat16
+I32 = mybir.dt.int32
+U32 = mybir.dt.uint32
+U8 = mybir.dt.uint8
+FP8X4 = mybir.dt.float8_e4m3fn_x4
+ACT = mybir.ActivationFunctionType
+ALU = mybir.AluOpType
+
+NODES, KIDS, H = 2048, 8, 256
+P = 128
+PACK = 4
+NODES_PER_PARTITION = NODES // P
+GROUP = 2
+ROUNDS = NODES_PER_PARTITION // GROUP
+COLS = GROUP * P
+HALVES = H // P
+GATES = 4
+F_GATE, I_GATE, O_GATE, U_GATE = 0, 1, 2, 3
+AHEAD = 2
+
+FLOPS = 2 * NODES * (2 * H) * (GATES * H)
+
+
+def tile_treelstmcellv2_kernel(
+    tc,
+    mailbox_h,
+    mailbox_c,
+    U_iou_w_words,
+    U_iou_w_scales,
+    b_iou,
+    U_f_w_words,
+    U_f_w_scales,
+    U_f_b,
+    out,
+):
+    nc = tc.nc
+    h_rows = mailbox_h.rearrange("(p t) k h -> p t k h", t=NODES_PER_PARTITION)
+    c_rows = mailbox_c.rearrange("(p t) k h -> p t k h", t=NODES_PER_PARTITION)
+    out_rows = out.rearrange("(p t) f -> p t f", t=NODES_PER_PARTITION)
+
+    with ExitStack() as ctx:
+        keep = ctx.enter_context(tc.tile_pool(name="keep", bufs=1))
+        loads = ctx.enter_context(tc.tile_pool(name="loads", bufs=AHEAD + 2))
+        work = ctx.enter_context(tc.tile_pool(name="work", bufs=2))
+        psum_one = ctx.enter_context(tc.psum_pool(name="psum_one", bufs=1))
+        psum_gate = ctx.enter_context(tc.psum_pool(name="psum_gate", bufs=GATES))
+
+        h_tiles, c_tiles = {}, {}
+
+        def load(g):
+            rows = slice(g * GROUP, (g + 1) * GROUP)
+            h_sb = loads.tile([P, GROUP, KIDS, H], BF16)
+            nc.sync.dma_start(out=h_sb[:], in_=h_rows[:, rows])
+            c_sb = loads.tile([P, GROUP, KIDS, H], BF16)
+            nc.sync.dma_start(out=c_sb[:], in_=c_rows[:, rows])
+            h_tiles[g], c_tiles[g] = h_sb, c_sb
+
+        load(0)
+
+        ident_f32 = keep.tile([P, P], F32)
+        make_identity(nc, ident_f32[:])
+        ident_bf16 = keep.tile([P, P], BF16)
+        make_identity(nc, ident_bf16[:])
+
+        w_words = keep.tile([P, GATES * H], U32, align_bytes=64)
+        nc.sync.dma_start(
+            out=w_words[:, 0:H].bitcast(I32),
+            in_=U_f_w_words.rearrange("g p n t -> (g p) (n t)").bitcast(I32),
+        )
+        nc.sync.dma_start(
+            out=w_words[:, H : GATES * H].bitcast(I32),
+            in_=U_iou_w_words.rearrange("g p n t -> (g p) (n t)").bitcast(I32),
+        )
+        w_scales = keep.tile([P, GATES * H], U8, align_bytes=64)
+        nc.vector.memset(w_scales[:].bitcast(I32), 0)
+        f_scale_rows = U_f_w_scales.rearrange("g q n -> (g q) n")
+        iou_scale_rows = U_iou_w_scales.rearrange("g q n -> (g q) n")
+        for quadrant in range(4):
+            live = slice(32 * quadrant, 32 * quadrant + 4)
+            rows = slice(4 * quadrant, 4 * quadrant + 4)
+            nc.sync.dma_start(out=w_scales[live, 0:H].bitcast(I32), in_=f_scale_rows[rows, :].bitcast(I32))
+            nc.sync.dma_start(
+                out=w_scales[live, H : GATES * H].bitcast(I32), in_=iou_scale_rows[rows, :].bitcast(I32)
+            )
+
+        bias_rows = keep.tile([P, P], BF16)
+        nc.vector.memset(bias_rows[:], 0.0)
+        nc.sync.dma_start(out=bias_rows[0:HALVES, :], in_=U_f_b.rearrange("(j m) -> j m", m=P))
+        nc.sync.dma_start(
+            out=bias_rows[HALVES : GATES * HALVES, :], in_=b_iou.rearrange("o (j m) -> (o j) m", m=P)
+        )
+        bias_ps = psum_one.tile([P, P], BF16, tag="hcT_ps")
+        nc.tensor.transpose(bias_ps[:], bias_rows[:], ident_bf16[:])
+        bias_cols = keep.tile([P, GATES * HALVES], F32)
+        nc.vector.tensor_copy(out=bias_cols[:], in_=bias_ps[:, 0 : GATES * HALVES])
+
+        for g in range(1, AHEAD):
+            load(g)
+
+        hc_tiles, hcT_tiles, hq_tiles, cf_tiles, csT_tiles = {}, {}, {}, {}, {}
+        gate_tiles, prod_tiles, back_tiles, out_tiles = {}, {}, {}, {}
+
+        def max_tree(g):
+            h_sb = h_tiles[g]
+            hc = work.tile([P, GROUP, 2 * H], BF16)
+            max4 = work.tile([P, GROUP, 4, H], BF16)
+            nc.vector.tensor_tensor(out=max4[:], in0=h_sb[:, :, 0:4, :], in1=h_sb[:, :, 4:8, :], op=ALU.max)
+            max2 = work.tile([P, GROUP, 2, H], BF16)
+            nc.vector.tensor_tensor(out=max2[:], in0=max4[:, :, 0:2, :], in1=max4[:, :, 2:4, :], op=ALU.max)
+            nc.vector.tensor_tensor(out=hc[:, :, H : 2 * H], in0=max2[:, :, 0, :], in1=max2[:, :, 1, :], op=ALU.max)
+            hc_tiles[g] = hc
+
+        def sum_tree(g):
+            h_sb, hc = h_tiles[g], hc_tiles[g]
+            sum4 = work.tile([P, GROUP, 4, H], F32)
+            nc.vector.tensor_tensor(out=sum4[:], in0=h_sb[:, :, 0:4, :], in1=h_sb[:, :, 4:8, :], op=ALU.add)
+            sum2 = work.tile([P, GROUP, 2, H], F32)
+            nc.vector.tensor_tensor(out=sum2[:], in0=sum4[:, :, 0:2, :], in1=sum4[:, :, 2:4, :], op=ALU.add)
+            nc.vector.tensor_tensor(out=hc[:, :, 0:H], in0=sum2[:, :, 0, :], in1=sum2[:, :, 1, :], op=ALU.add)
+
+        def transpose_hc(g):
+            hc = hc_tiles[g]
+            hcT_ps = psum_one.tile([P, GROUP, PACK, P], BF16)
+            for j in range(GROUP):
+                for t in range(PACK):
+                    nc.tensor.transpose(hcT_ps[:, j, t, :], hc[:, j, t : 2 * H : PACK], ident_bf16[:])
+            hcT_tiles[g] = hcT_ps
+
+        def regroup_hc(g):
+            hcT = work.tile([P, GROUP, P, PACK], BF16, align_bytes=64)
+            nc.scalar.copy(out=hcT[:], in_=hcT_tiles[g][:].rearrange("p j t r -> p j r t"))
+            hcT_tiles[g] = hcT
+
+        def quantise_hc(g):
+            hq_words = work.tile([P, COLS], U32, align_bytes=64)
+            hq_scales = work.tile([P, COLS], U8, align_bytes=64)
+            nc.vector.quantize_mx(
+                out=hq_words[:].bitcast(FP8X4),
+                scales=hq_scales[:],
+                in_=hcT_tiles[g][:].rearrange("p j r t -> p (j r t)"),
+            )
+            hq_tiles[g] = (hq_words, hq_scales)
+
+        def widen_c(g):
+            c_f32 = work.tile([P, GROUP, KIDS, H], F32)
+            nc.scalar.copy(out=c_f32[:], in_=c_tiles[g][:])
+            cf_tiles[g] = c_f32
+
+        def sum_c(g):
+            c_f32 = cf_tiles[g]
+            csT_ps = psum_one.tile([P, HALVES, COLS], F32)
+            for half in range(HALVES):
+                for j in range(GROUP):
+                    for kid in range(KIDS):
+                        nc.tensor.matmul(
+                            out=csT_ps[:, half, j * P : (j + 1) * P],
+                            lhsT=c_f32[:, j, kid, half * P : (half + 1) * P],
+                            rhs=ident_f32[:],
+                            is_transpose=True,
+                            start=(kid == 0),
+                            stop=(kid == KIDS - 1),
+                        )
+            csT_tiles[g] = csT_ps
+
+        def gates(g):
+            hq_words, hq_scales = hq_tiles[g]
+            banks = []
+            for gate in range(GATES):
+                gate_ps = psum_gate.tile([P, HALVES, COLS], F32)
+                for half in range(HALVES):
+                    cols = slice((gate * HALVES + half) * P, (gate * HALVES + half + 1) * P)
+                    nc.tensor.matmul_mx(
+                        out=gate_ps[:, half, :],
+                        lhsT=w_words[:, cols].bitcast(FP8X4),
+                        lhsT_scale=w_scales[:, cols],
+                        rhs=hq_words[:].bitcast(FP8X4),
+                        rhs_scale=hq_scales[:],
+                        start=True,
+                        stop=True,
+                    )
+                banks.append(gate_ps)
+            acts = []
+            for gate in range(GATES):
+                gate_sb = work.tile([P, HALVES, COLS], F32, name="gate_sb_%d" % gate)
+                for half in range(HALVES):
+                    column = gate * HALVES + half
+                    nc.scalar.activation(
+                        out=gate_sb[:, half, :],
+                        in_=banks[gate][:, half, :],
+                        func=ACT.Tanh if gate == U_GATE else ACT.Sigmoid,
+                        bias=bias_cols[:, column : column + 1],
+                        scale=1.0,
+                    )
+                acts.append(gate_sb)
+            gate_tiles[g] = acts
+
+        def products(g):
+            acts = gate_tiles[g]
+            iu = work.tile([P, HALVES, COLS], F32)
+            nc.vector.tensor_tensor(out=iu[:], in0=acts[I_GATE][:], in1=acts[U_GATE][:], op=ALU.mult)
+            fc = work.tile([P, HALVES, COLS], F32)
+            nc.vector.tensor_tensor(out=fc[:], in0=acts[F_GATE][:], in1=csT_tiles[g][:], op=ALU.mult)
+            prod_tiles[g] = (iu, fc)
+
+        def transpose_back(g):
+            iu, fc = prod_tiles[g]
+            o_sb = gate_tiles[g][O_GATE]
+            c_ps = psum_one.tile([P, GROUP, H], F32)
+            o_ps = psum_one.tile([P, GROUP, H], F32)
+            for j in range(GROUP):
+                for half in range(HALVES):
+                    nodes = slice(j * P, (j + 1) * P)
+                    feats = slice(half * P, (half + 1) * P)
+                    nc.tensor.matmul(
+                        out=c_ps[:, j, feats], lhsT=iu[:, half, nodes], rhs=ident_f32[:],
+                        is_transpose=True, start=True, stop=False,
+                    )
+                    nc.tensor.matmul(
+                        out=c_ps[:, j, feats], lhsT=fc[:, half, nodes], rhs=ident_f32[:],
+                        is_transpose=True, start=False, stop=True,
+                    )
+                    nc.tensor.transpose(o_ps[:, j, feats], o_sb[:, half, nodes], ident_f32[:])
+            back_tiles[g] = (c_ps, o_ps)
+
+        def finish_c(g):
+            c_ps, o_ps = back_tiles[g]
+            out_sb = work.tile([P, GROUP, 2 * H], F32)
+            nc.scalar.copy(out=out_sb[:, :, H : 2 * H], in_=c_ps[:])
+            tanh_c = work.tile([P, GROUP, H], F32)
+            nc.scalar.activation(out=tanh_c[:], in_=c_ps[:], func=ACT.Tanh)
+            out_tiles[g] = (out_sb, tanh_c)
+
+        def finish_h(g):
+            c_ps, o_ps = back_tiles[g]
+            out_sb, tanh_c = out_tiles[g]
+            nc.vector.tensor_tensor(out=out_sb[:, :, 0:H], in0=o_ps[:], in1=tanh_c[:], op=ALU.mult)
+            nc.sync.dma_start(out=out_rows[:, g * GROUP : (g + 1) * GROUP], in_=out_sb[:])
+
+        for step in range(ROUNDS + 2):
+            first, middle, last = step, step - 1, step - 2
+            if first + AHEAD < ROUNDS:
+                load(first + AHEAD)
+            if first < ROUNDS:
+                max_tree(first)
+            if 0 <= last:
+                transpose_back(last)
+            if 0 <= middle < ROUNDS:
+                regroup_hc(middle)
+                quantise_hc(middle)
+            if 0 <= last:
+                finish_c(last)
+                finish_h(last)
+            if 0 <= middle < ROUNDS:
+                sum_c(middle)
+                gates(middle)
+            if first < ROUNDS:
+                sum_tree(first)
+                transpose_hc(first)
+                widen_c(first)
+            if 0 <= middle < ROUNDS:
+                products(middle)

@@ -23,6 +23,7 @@ HALVES = H // P
 GATES = 4
 F_GATE, I_GATE, O_GATE, U_GATE = 0, 1, 2, 3
 AHEAD = 2
+KIDS_WIDENED = 6
 
 FLOPS = 2 * NODES * (2 * H) * (GATES * H)
 
@@ -103,7 +104,7 @@ def tile_treelstmcellv2_kernel(
         for g in range(1, AHEAD):
             load(g)
 
-        hc_tiles, hcT_tiles, hq_tiles, cf_tiles, csT_tiles = {}, {}, {}, {}, {}
+        hc_tiles, hcT_tiles, hq_tiles, wide_tiles, pair_tiles, csT_tiles = {}, {}, {}, {}, {}, {}
         gate_tiles, prod_tiles, back_tiles, out_tiles = {}, {}, {}, {}
 
         def max_tree(g):
@@ -147,24 +148,34 @@ def tile_treelstmcellv2_kernel(
             )
             hq_tiles[g] = (hq_words, hq_scales)
 
+        def pair_c(g):
+            c_sb = c_tiles[g]
+            c_pair = work.tile([P, GROUP, H], F32)
+            nc.vector.tensor_tensor(
+                out=c_pair[:], in0=c_sb[:, :, KIDS_WIDENED, :], in1=c_sb[:, :, KIDS_WIDENED + 1, :], op=ALU.add
+            )
+            pair_tiles[g] = c_pair
+
         def widen_c(g):
-            c_f32 = work.tile([P, GROUP, KIDS, H], F32)
-            nc.scalar.copy(out=c_f32[:], in_=c_tiles[g][:])
-            cf_tiles[g] = c_f32
+            c_wide = work.tile([P, GROUP, KIDS_WIDENED, H], F32)
+            nc.scalar.copy(out=c_wide[:], in_=c_tiles[g][:, :, 0:KIDS_WIDENED, :])
+            wide_tiles[g] = c_wide
 
         def sum_c(g):
-            c_f32 = cf_tiles[g]
+            c_wide, c_pair = wide_tiles[g], pair_tiles[g]
             csT_ps = psum_one.tile([P, HALVES, COLS], F32)
             for half in range(HALVES):
+                feats = slice(half * P, (half + 1) * P)
                 for j in range(GROUP):
-                    for kid in range(KIDS):
+                    terms = [c_wide[:, j, kid, feats] for kid in range(KIDS_WIDENED)] + [c_pair[:, j, feats]]
+                    for n, term in enumerate(terms):
                         nc.tensor.matmul(
                             out=csT_ps[:, half, j * P : (j + 1) * P],
-                            lhsT=c_f32[:, j, kid, half * P : (half + 1) * P],
+                            lhsT=term,
                             rhs=ident_f32[:],
                             is_transpose=True,
-                            start=(kid == 0),
-                            stop=(kid == KIDS - 1),
+                            start=(n == 0),
+                            stop=(n == len(terms) - 1),
                         )
             csT_tiles[g] = csT_ps
 
@@ -242,26 +253,28 @@ def tile_treelstmcellv2_kernel(
             nc.vector.tensor_tensor(out=out_sb[:, :, 0:H], in0=o_ps[:], in1=tanh_c[:], op=ALU.mult)
             nc.sync.dma_start(out=out_rows[:, g * GROUP : (g + 1) * GROUP], in_=out_sb[:])
 
-        for step in range(ROUNDS + 2):
-            first, middle, last = step, step - 1, step - 2
-            if first + AHEAD < ROUNDS:
-                load(first + AHEAD)
-            if first < ROUNDS:
-                max_tree(first)
-            if 0 <= last:
-                transpose_back(last)
-            if 0 <= middle < ROUNDS:
-                regroup_hc(middle)
-                quantise_hc(middle)
-            if 0 <= last:
-                finish_c(last)
-                finish_h(last)
-            if 0 <= middle < ROUNDS:
-                sum_c(middle)
-                gates(middle)
-            if first < ROUNDS:
-                sum_tree(first)
-                transpose_hc(first)
-                widen_c(first)
-            if 0 <= middle < ROUNDS:
-                products(middle)
+        with tc.manual_schedule():
+            for step in range(ROUNDS + 2):
+                first, middle, last = step, step - 1, step - 2
+                if first + AHEAD < ROUNDS:
+                    load(first + AHEAD)
+                if first < ROUNDS:
+                    max_tree(first)
+                if 0 <= last:
+                    transpose_back(last)
+                if 0 <= middle < ROUNDS:
+                    regroup_hc(middle)
+                    quantise_hc(middle)
+                if 0 <= last:
+                    finish_c(last)
+                    finish_h(last)
+                if 0 <= middle < ROUNDS:
+                    gates(middle)
+                    sum_c(middle)
+                if first < ROUNDS:
+                    sum_tree(first)
+                    pair_c(first)
+                    transpose_hc(first)
+                    widen_c(first)
+                if 0 <= middle < ROUNDS:
+                    products(middle)

@@ -104,26 +104,31 @@ def tile_treelstmcellv2_kernel(
         for g in range(1, AHEAD):
             load(g)
 
-        hc_tiles, hcT_tiles, hq_tiles, wide_tiles, pair_tiles, csT_tiles = {}, {}, {}, {}, {}, {}
-        gate_tiles, prod_tiles, back_tiles, out_tiles = {}, {}, {}, {}
+        tree_tiles, hc_tiles, hcT_tiles, hq_tiles, wide_tiles, pair_tiles, csT_tiles = {}, {}, {}, {}, {}, {}, {}
+        bank_tiles, gate_tiles, prod_tiles, back_tiles, out_tiles = {}, {}, {}, {}, {}
 
-        def max_tree(g):
+        def tree_level_1(g):
             h_sb = h_tiles[g]
-            hc = work.tile([P, GROUP, 2 * H], BF16)
             max4 = work.tile([P, GROUP, 4, H], BF16)
             nc.vector.tensor_tensor(out=max4[:], in0=h_sb[:, :, 0:4, :], in1=h_sb[:, :, 4:8, :], op=ALU.max)
-            max2 = work.tile([P, GROUP, 2, H], BF16)
-            nc.vector.tensor_tensor(out=max2[:], in0=max4[:, :, 0:2, :], in1=max4[:, :, 2:4, :], op=ALU.max)
-            nc.vector.tensor_tensor(out=hc[:, :, H : 2 * H], in0=max2[:, :, 0, :], in1=max2[:, :, 1, :], op=ALU.max)
-            hc_tiles[g] = hc
-
-        def sum_tree(g):
-            h_sb, hc = h_tiles[g], hc_tiles[g]
             sum4 = work.tile([P, GROUP, 4, H], F32)
             nc.vector.tensor_tensor(out=sum4[:], in0=h_sb[:, :, 0:4, :], in1=h_sb[:, :, 4:8, :], op=ALU.add)
+            tree_tiles[g] = (max4, sum4)
+
+        def tree_level_2(g):
+            max4, sum4 = tree_tiles[g]
+            max2 = work.tile([P, GROUP, 2, H], BF16)
+            nc.vector.tensor_tensor(out=max2[:], in0=max4[:, :, 0:2, :], in1=max4[:, :, 2:4, :], op=ALU.max)
             sum2 = work.tile([P, GROUP, 2, H], F32)
             nc.vector.tensor_tensor(out=sum2[:], in0=sum4[:, :, 0:2, :], in1=sum4[:, :, 2:4, :], op=ALU.add)
+            tree_tiles[g] = (max2, sum2)
+
+        def tree_level_3(g):
+            max2, sum2 = tree_tiles[g]
+            hc = work.tile([P, GROUP, 2 * H], BF16)
+            nc.vector.tensor_tensor(out=hc[:, :, H : 2 * H], in0=max2[:, :, 0, :], in1=max2[:, :, 1, :], op=ALU.max)
             nc.vector.tensor_tensor(out=hc[:, :, 0:H], in0=sum2[:, :, 0, :], in1=sum2[:, :, 1, :], op=ALU.add)
+            hc_tiles[g] = hc
 
         def transpose_hc(g):
             hc = hc_tiles[g]
@@ -156,30 +161,31 @@ def tile_treelstmcellv2_kernel(
             )
             pair_tiles[g] = c_pair
 
-        def widen_c(g):
-            c_wide = work.tile([P, GROUP, KIDS_WIDENED, H], F32)
-            nc.scalar.copy(out=c_wide[:], in_=c_tiles[g][:, :, 0:KIDS_WIDENED, :])
-            wide_tiles[g] = c_wide
+        def widen_c(g, j):
+            if j == 0:
+                c_wide = work.tile([P, GROUP, KIDS_WIDENED, H], F32)
+                wide_tiles[g] = c_wide
+            nc.scalar.copy(out=wide_tiles[g][:, j], in_=c_tiles[g][:, j, 0:KIDS_WIDENED, :])
 
-        def sum_c(g):
+        def sum_c(g, half):
             c_wide, c_pair = wide_tiles[g], pair_tiles[g]
-            csT_ps = psum_one.tile([P, HALVES, COLS], F32)
-            for half in range(HALVES):
-                feats = slice(half * P, (half + 1) * P)
-                for j in range(GROUP):
-                    terms = [c_wide[:, j, kid, feats] for kid in range(KIDS_WIDENED)] + [c_pair[:, j, feats]]
-                    for n, term in enumerate(terms):
-                        nc.tensor.matmul(
-                            out=csT_ps[:, half, j * P : (j + 1) * P],
-                            lhsT=term,
-                            rhs=ident_f32[:],
-                            is_transpose=True,
-                            start=(n == 0),
-                            stop=(n == len(terms) - 1),
-                        )
-            csT_tiles[g] = csT_ps
+            if half == 0:
+                csT_ps = psum_one.tile([P, HALVES, COLS], F32)
+                csT_tiles[g] = csT_ps
+            feats = slice(half * P, (half + 1) * P)
+            for j in range(GROUP):
+                terms = [c_wide[:, j, kid, feats] for kid in range(KIDS_WIDENED)] + [c_pair[:, j, feats]]
+                for n, term in enumerate(terms):
+                    nc.tensor.matmul(
+                        out=csT_tiles[g][:, half, j * P : (j + 1) * P],
+                        lhsT=term,
+                        rhs=ident_f32[:],
+                        is_transpose=True,
+                        start=(n == 0),
+                        stop=(n == len(terms) - 1),
+                    )
 
-        def gates(g):
+        def gate_products(g):
             hq_words, hq_scales = hq_tiles[g]
             banks = []
             for gate in range(GATES):
@@ -196,22 +202,25 @@ def tile_treelstmcellv2_kernel(
                         stop=True,
                     )
                 banks.append(gate_ps)
-            acts = []
-            for gate in range(GATES):
+            bank_tiles[g] = banks
+
+        def gate_activations(g):
+            acts = {}
+            for gate in (I_GATE, U_GATE, F_GATE, O_GATE):
                 gate_sb = work.tile([P, HALVES, COLS], F32, name="gate_sb_%d" % gate)
                 for half in range(HALVES):
                     column = gate * HALVES + half
                     nc.scalar.activation(
                         out=gate_sb[:, half, :],
-                        in_=banks[gate][:, half, :],
+                        in_=bank_tiles[g][gate][:, half, :],
                         func=ACT.Tanh if gate == U_GATE else ACT.Sigmoid,
                         bias=bias_cols[:, column : column + 1],
                         scale=1.0,
                     )
-                acts.append(gate_sb)
+                acts[gate] = gate_sb
             gate_tiles[g] = acts
 
-        def products(g):
+        def multiply(g):
             acts = gate_tiles[g]
             iu = work.tile([P, HALVES, COLS], F32)
             nc.vector.tensor_tensor(out=iu[:], in0=acts[I_GATE][:], in1=acts[U_GATE][:], op=ALU.mult)
@@ -253,28 +262,41 @@ def tile_treelstmcellv2_kernel(
             nc.vector.tensor_tensor(out=out_sb[:, :, 0:H], in0=o_ps[:], in1=tanh_c[:], op=ALU.mult)
             nc.sync.dma_start(out=out_rows[:, g * GROUP : (g + 1) * GROUP], in_=out_sb[:])
 
+        def live(g):
+            return 0 <= g < ROUNDS
+
         with tc.manual_schedule():
-            for step in range(ROUNDS + 2):
-                first, middle, last = step, step - 1, step - 2
-                if first + AHEAD < ROUNDS:
-                    load(first + AHEAD)
-                if first < ROUNDS:
-                    max_tree(first)
-                if 0 <= last:
-                    transpose_back(last)
-                if 0 <= middle < ROUNDS:
-                    regroup_hc(middle)
-                    quantise_hc(middle)
-                if 0 <= last:
-                    finish_c(last)
-                    finish_h(last)
-                if 0 <= middle < ROUNDS:
-                    gates(middle)
-                    sum_c(middle)
-                if first < ROUNDS:
-                    sum_tree(first)
-                    pair_c(first)
-                    transpose_hc(first)
-                    widen_c(first)
-                if 0 <= middle < ROUNDS:
-                    products(middle)
+            for step in range(ROUNDS + 3):
+                a, b, c, d = step, step - 1, step - 2, step - 3
+                if live(a + AHEAD):
+                    load(a + AHEAD)
+                if live(d):
+                    finish_h(d)
+                if live(c):
+                    multiply(c)
+                if live(b):
+                    transpose_hc(b)
+                if live(a):
+                    widen_c(a, 0)
+                if live(b):
+                    regroup_hc(b)
+                if live(a):
+                    tree_level_1(a)
+                if live(b):
+                    quantise_hc(b)
+                if live(c):
+                    transpose_back(c)
+                if live(b):
+                    sum_c(b, 0)
+                    gate_products(b)
+                    sum_c(b, 1)
+                if live(a):
+                    widen_c(a, 1)
+                if live(c):
+                    finish_c(c)
+                if live(b):
+                    gate_activations(b)
+                if live(a):
+                    tree_level_2(a)
+                    tree_level_3(a)
+                    pair_c(a)

@@ -16,14 +16,16 @@ NODES, KIDS, H = 2048, 8, 256
 P = 128
 PACK = 4
 NODES_PER_PARTITION = NODES // P
-GROUP = 2
-ROUNDS = NODES_PER_PARTITION // GROUP
-COLS = GROUP * P
 HALVES = H // P
 GATES = 4
 F_GATE, I_GATE, O_GATE, U_GATE = 0, 1, 2, 3
+WIDTHS = [1, 1] + [2] * (NODES_PER_PARTITION // 2 - 2) + [1, 1]
+ROUNDS = len(WIDTHS)
+STARTS = [sum(WIDTHS[:g]) for g in range(ROUNDS)]
+assert sum(WIDTHS) == NODES_PER_PARTITION
 AHEAD = 2
-KIDS_WIDENED = 6
+NODES_PER_BLOCK = P // KIDS
+BLOCKS = P // NODES_PER_BLOCK
 
 FLOPS = 2 * NODES * (2 * H) * (GATES * H)
 
@@ -41,9 +43,9 @@ def tile_treelstmcellv2_kernel(
     out,
 ):
     nc = tc.nc
-    h_rows = mailbox_h.rearrange("(p t) k h -> p t k h", t=NODES_PER_PARTITION)
-    c_rows = mailbox_c.rearrange("(p t) k h -> p t k h", t=NODES_PER_PARTITION)
-    out_rows = out.rearrange("(p t) f -> p t f", t=NODES_PER_PARTITION)
+    h_rows = mailbox_h.rearrange("(t p) k h -> p t k h", p=P)
+    c_rows = mailbox_c.rearrange("(t q n) k h -> (n k) t q h", q=BLOCKS, n=NODES_PER_BLOCK)
+    out_rows = out.rearrange("(t p) f -> p t f", p=P)
 
     with ExitStack() as ctx:
         keep = ctx.enter_context(tc.tile_pool(name="keep", bufs=1))
@@ -55,10 +57,10 @@ def tile_treelstmcellv2_kernel(
         h_tiles, c_tiles = {}, {}
 
         def load(g):
-            rows = slice(g * GROUP, (g + 1) * GROUP)
-            h_sb = loads.tile([P, GROUP, KIDS, H], BF16)
+            rows = slice(STARTS[g], STARTS[g] + WIDTHS[g])
+            h_sb = loads.tile([P, WIDTHS[g], KIDS, H], BF16)
             nc.sync.dma_start(out=h_sb[:], in_=h_rows[:, rows])
-            c_sb = loads.tile([P, GROUP, KIDS, H], BF16)
+            c_sb = loads.tile([P, WIDTHS[g], BLOCKS, H], BF16)
             nc.sync.dma_start(out=c_sb[:], in_=c_rows[:, rows])
             h_tiles[g], c_tiles[g] = h_sb, c_sb
 
@@ -68,6 +70,14 @@ def tile_treelstmcellv2_kernel(
         make_identity(nc, ident_f32[:])
         ident_bf16 = keep.tile([P, P], BF16)
         make_identity(nc, ident_bf16[:])
+        add_kids = keep.tile([P, NODES_PER_BLOCK], BF16)
+        with nc.allow_low_precision(reason="sums of one 1 and seven 0s are exact"):
+            nc.vector.tensor_reduce(
+                out=add_kids[:],
+                in_=ident_bf16[:].rearrange("p (n k) -> p n k", k=KIDS),
+                axis=mybir.AxisListType.X,
+                op=ALU.add,
+            )
 
         w_words = keep.tile([P, GATES * H], U32, align_bytes=64)
         nc.sync.dma_start(
@@ -83,11 +93,13 @@ def tile_treelstmcellv2_kernel(
         f_scale_rows = U_f_w_scales.rearrange("g q n -> (g q) n")
         iou_scale_rows = U_iou_w_scales.rearrange("g q n -> (g q) n")
         for quadrant in range(4):
-            live = slice(32 * quadrant, 32 * quadrant + 4)
+            live_rows = slice(32 * quadrant, 32 * quadrant + 4)
             rows = slice(4 * quadrant, 4 * quadrant + 4)
-            nc.sync.dma_start(out=w_scales[live, 0:H].bitcast(I32), in_=f_scale_rows[rows, :].bitcast(I32))
             nc.sync.dma_start(
-                out=w_scales[live, H : GATES * H].bitcast(I32), in_=iou_scale_rows[rows, :].bitcast(I32)
+                out=w_scales[live_rows, 0:H].bitcast(I32), in_=f_scale_rows[rows, :].bitcast(I32)
+            )
+            nc.sync.dma_start(
+                out=w_scales[live_rows, H : GATES * H].bitcast(I32), in_=iou_scale_rows[rows, :].bitcast(I32)
             )
 
         bias_rows = keep.tile([P, P], BF16)
@@ -104,48 +116,43 @@ def tile_treelstmcellv2_kernel(
         for g in range(1, AHEAD):
             load(g)
 
-        tree_tiles, hc_tiles, hcT_tiles, hq_tiles, wide_tiles, pair_tiles, csT_tiles = {}, {}, {}, {}, {}, {}, {}
-        bank_tiles, gate_tiles, prod_tiles, back_tiles, out_tiles = {}, {}, {}, {}, {}
+        tree_tiles, hc_tiles, hcT_banks, hcT_tiles, hq_tiles = {}, {}, {}, {}, {}
+        csT_banks = {}
+        gate_banks, gate_tiles, prod_tiles, back_banks, out_tiles = {}, {}, {}, {}, {}
 
-        def tree_level_1(g):
-            h_sb = h_tiles[g]
-            max4 = work.tile([P, GROUP, 4, H], BF16)
-            nc.vector.tensor_tensor(out=max4[:], in0=h_sb[:, :, 0:4, :], in1=h_sb[:, :, 4:8, :], op=ALU.max)
-            sum4 = work.tile([P, GROUP, 4, H], F32)
-            nc.vector.tensor_tensor(out=sum4[:], in0=h_sb[:, :, 0:4, :], in1=h_sb[:, :, 4:8, :], op=ALU.add)
-            tree_tiles[g] = (max4, sum4)
+        trees = {"sum": (ALU.add, F32, 0), "max": (ALU.max, BF16, H)}
 
-        def tree_level_2(g):
-            max4, sum4 = tree_tiles[g]
-            max2 = work.tile([P, GROUP, 2, H], BF16)
-            nc.vector.tensor_tensor(out=max2[:], in0=max4[:, :, 0:2, :], in1=max4[:, :, 2:4, :], op=ALU.max)
-            sum2 = work.tile([P, GROUP, 2, H], F32)
-            nc.vector.tensor_tensor(out=sum2[:], in0=sum4[:, :, 0:2, :], in1=sum4[:, :, 2:4, :], op=ALU.add)
-            tree_tiles[g] = (max2, sum2)
-
-        def tree_level_3(g):
-            max2, sum2 = tree_tiles[g]
-            hc = work.tile([P, GROUP, 2 * H], BF16)
-            nc.vector.tensor_tensor(out=hc[:, :, H : 2 * H], in0=max2[:, :, 0, :], in1=max2[:, :, 1, :], op=ALU.max)
-            nc.vector.tensor_tensor(out=hc[:, :, 0:H], in0=sum2[:, :, 0, :], in1=sum2[:, :, 1, :], op=ALU.add)
-            hc_tiles[g] = hc
+        def halve(g, tree, kids):
+            op, dtype, column = trees[tree]
+            src = tree_tiles.get((g, tree), h_tiles[g])
+            if kids > 1:
+                dst = work.tile([P, WIDTHS[g], kids, H], dtype, name="%s_%d" % (tree, kids))
+                nc.vector.tensor_tensor(out=dst[:], in0=src[:, :, 0:kids, :], in1=src[:, :, kids : 2 * kids, :], op=op)
+                tree_tiles[(g, tree)] = dst
+            else:
+                if g not in hc_tiles:
+                    hc = work.tile([P, WIDTHS[g], 2 * H], BF16)
+                    hc_tiles[g] = hc
+                nc.vector.tensor_tensor(
+                    out=hc_tiles[g][:, :, column : column + H], in0=src[:, :, 0, :], in1=src[:, :, 1, :], op=op
+                )
 
         def transpose_hc(g):
             hc = hc_tiles[g]
-            hcT_ps = psum_one.tile([P, GROUP, PACK, P], BF16)
-            for j in range(GROUP):
+            hcT_ps = psum_one.tile([P, WIDTHS[g], PACK, P], BF16)
+            for j in range(WIDTHS[g]):
                 for t in range(PACK):
                     nc.tensor.transpose(hcT_ps[:, j, t, :], hc[:, j, t : 2 * H : PACK], ident_bf16[:])
-            hcT_tiles[g] = hcT_ps
+            hcT_banks[g] = hcT_ps
 
         def regroup_hc(g):
-            hcT = work.tile([P, GROUP, P, PACK], BF16, align_bytes=64)
-            nc.scalar.copy(out=hcT[:], in_=hcT_tiles[g][:].rearrange("p j t r -> p j r t"))
+            hcT = work.tile([P, WIDTHS[g], P, PACK], BF16, align_bytes=64)
+            nc.scalar.copy(out=hcT[:], in_=hcT_banks[g][:].rearrange("p j t r -> p j r t"))
             hcT_tiles[g] = hcT
 
         def quantise_hc(g):
-            hq_words = work.tile([P, COLS], U32, align_bytes=64)
-            hq_scales = work.tile([P, COLS], U8, align_bytes=64)
+            hq_words = work.tile([P, WIDTHS[g] * P], U32, align_bytes=64)
+            hq_scales = work.tile([P, WIDTHS[g] * P], U8, align_bytes=64)
             nc.vector.quantize_mx(
                 out=hq_words[:].bitcast(FP8X4),
                 scales=hq_scales[:],
@@ -153,43 +160,27 @@ def tile_treelstmcellv2_kernel(
             )
             hq_tiles[g] = (hq_words, hq_scales)
 
-        def pair_c(g):
+        def sum_c(g):
             c_sb = c_tiles[g]
-            c_pair = work.tile([P, GROUP, H], F32)
-            nc.vector.tensor_tensor(
-                out=c_pair[:], in0=c_sb[:, :, KIDS_WIDENED, :], in1=c_sb[:, :, KIDS_WIDENED + 1, :], op=ALU.add
-            )
-            pair_tiles[g] = c_pair
-
-        def widen_c(g, j):
-            if j == 0:
-                c_wide = work.tile([P, GROUP, KIDS_WIDENED, H], F32)
-                wide_tiles[g] = c_wide
-            nc.scalar.copy(out=wide_tiles[g][:, j], in_=c_tiles[g][:, j, 0:KIDS_WIDENED, :])
-
-        def sum_c(g, half):
-            c_wide, c_pair = wide_tiles[g], pair_tiles[g]
-            if half == 0:
-                csT_ps = psum_one.tile([P, HALVES, COLS], F32)
-                csT_tiles[g] = csT_ps
-            feats = slice(half * P, (half + 1) * P)
-            for j in range(GROUP):
-                terms = [c_wide[:, j, kid, feats] for kid in range(KIDS_WIDENED)] + [c_pair[:, j, feats]]
-                for n, term in enumerate(terms):
-                    nc.tensor.matmul(
-                        out=csT_tiles[g][:, half, j * P : (j + 1) * P],
-                        lhsT=term,
-                        rhs=ident_f32[:],
-                        is_transpose=True,
-                        start=(n == 0),
-                        stop=(n == len(terms) - 1),
-                    )
+            csT_ps = psum_one.tile([P, HALVES, WIDTHS[g] * P], F32)
+            for half in range(HALVES):
+                for j in range(WIDTHS[g]):
+                    for q in range(BLOCKS):
+                        first = j * P + q * NODES_PER_BLOCK
+                        nc.tensor.matmul(
+                            out=csT_ps[:, half, first : first + NODES_PER_BLOCK],
+                            lhsT=c_sb[:, j, q, half * P : (half + 1) * P],
+                            rhs=add_kids[:],
+                            start=True,
+                            stop=True,
+                        )
+            csT_banks[g] = csT_ps
 
         def gate_products(g):
             hq_words, hq_scales = hq_tiles[g]
             banks = []
             for gate in range(GATES):
-                gate_ps = psum_gate.tile([P, HALVES, COLS], F32)
+                gate_ps = psum_gate.tile([P, HALVES, WIDTHS[g] * P], F32)
                 for half in range(HALVES):
                     cols = slice((gate * HALVES + half) * P, (gate * HALVES + half + 1) * P)
                     nc.tensor.matmul_mx(
@@ -202,17 +193,17 @@ def tile_treelstmcellv2_kernel(
                         stop=True,
                     )
                 banks.append(gate_ps)
-            bank_tiles[g] = banks
+            gate_banks[g] = banks
 
         def gate_activations(g):
             acts = {}
             for gate in (I_GATE, U_GATE, F_GATE, O_GATE):
-                gate_sb = work.tile([P, HALVES, COLS], F32, name="gate_sb_%d" % gate)
+                gate_sb = work.tile([P, HALVES, WIDTHS[g] * P], F32, name="gate_sb_%d" % gate)
                 for half in range(HALVES):
                     column = gate * HALVES + half
                     nc.scalar.activation(
                         out=gate_sb[:, half, :],
-                        in_=bank_tiles[g][gate][:, half, :],
+                        in_=gate_banks[g][gate][:, half, :],
                         func=ACT.Tanh if gate == U_GATE else ACT.Sigmoid,
                         bias=bias_cols[:, column : column + 1],
                         scale=1.0,
@@ -222,18 +213,18 @@ def tile_treelstmcellv2_kernel(
 
         def multiply(g):
             acts = gate_tiles[g]
-            iu = work.tile([P, HALVES, COLS], F32)
+            iu = work.tile([P, HALVES, WIDTHS[g] * P], F32)
             nc.vector.tensor_tensor(out=iu[:], in0=acts[I_GATE][:], in1=acts[U_GATE][:], op=ALU.mult)
-            fc = work.tile([P, HALVES, COLS], F32)
-            nc.vector.tensor_tensor(out=fc[:], in0=acts[F_GATE][:], in1=csT_tiles[g][:], op=ALU.mult)
+            fc = work.tile([P, HALVES, WIDTHS[g] * P], F32)
+            nc.vector.tensor_tensor(out=fc[:], in0=acts[F_GATE][:], in1=csT_banks[g][:], op=ALU.mult)
             prod_tiles[g] = (iu, fc)
 
         def transpose_back(g):
             iu, fc = prod_tiles[g]
             o_sb = gate_tiles[g][O_GATE]
-            c_ps = psum_one.tile([P, GROUP, H], F32)
-            o_ps = psum_one.tile([P, GROUP, H], F32)
-            for j in range(GROUP):
+            c_ps = psum_one.tile([P, WIDTHS[g], H], F32)
+            o_ps = psum_one.tile([P, WIDTHS[g], H], F32)
+            for j in range(WIDTHS[g]):
                 for half in range(HALVES):
                     nodes = slice(j * P, (j + 1) * P)
                     feats = slice(half * P, (half + 1) * P)
@@ -246,21 +237,21 @@ def tile_treelstmcellv2_kernel(
                         is_transpose=True, start=False, stop=True,
                     )
                     nc.tensor.transpose(o_ps[:, j, feats], o_sb[:, half, nodes], ident_f32[:])
-            back_tiles[g] = (c_ps, o_ps)
+            back_banks[g] = (c_ps, o_ps)
 
         def finish_c(g):
-            c_ps, o_ps = back_tiles[g]
-            out_sb = work.tile([P, GROUP, 2 * H], F32)
+            c_ps, o_ps = back_banks[g]
+            out_sb = work.tile([P, WIDTHS[g], 2 * H], F32)
             nc.scalar.copy(out=out_sb[:, :, H : 2 * H], in_=c_ps[:])
-            tanh_c = work.tile([P, GROUP, H], F32)
+            tanh_c = work.tile([P, WIDTHS[g], H], F32)
             nc.scalar.activation(out=tanh_c[:], in_=c_ps[:], func=ACT.Tanh)
             out_tiles[g] = (out_sb, tanh_c)
 
         def finish_h(g):
-            c_ps, o_ps = back_tiles[g]
+            c_ps, o_ps = back_banks[g]
             out_sb, tanh_c = out_tiles[g]
             nc.vector.tensor_tensor(out=out_sb[:, :, 0:H], in0=o_ps[:], in1=tanh_c[:], op=ALU.mult)
-            nc.sync.dma_start(out=out_rows[:, g * GROUP : (g + 1) * GROUP], in_=out_sb[:])
+            nc.sync.dma_start(out=out_rows[:, STARTS[g] : STARTS[g] + WIDTHS[g]], in_=out_sb[:])
 
         def live(g):
             return 0 <= g < ROUNDS
@@ -276,27 +267,21 @@ def tile_treelstmcellv2_kernel(
                     multiply(c)
                 if live(b):
                     transpose_hc(b)
-                if live(a):
-                    widen_c(a, 0)
-                if live(b):
                     regroup_hc(b)
                 if live(a):
-                    tree_level_1(a)
+                    halve(a, "max", 4)
+                    halve(a, "sum", 4)
                 if live(b):
                     quantise_hc(b)
                 if live(c):
                     transpose_back(c)
-                if live(b):
-                    sum_c(b, 0)
-                    gate_products(b)
-                    sum_c(b, 1)
-                if live(a):
-                    widen_c(a, 1)
-                if live(c):
                     finish_c(c)
                 if live(b):
+                    sum_c(b)
+                    gate_products(b)
                     gate_activations(b)
                 if live(a):
-                    tree_level_2(a)
-                    tree_level_3(a)
-                    pair_c(a)
+                    halve(a, "max", 2)
+                    halve(a, "sum", 2)
+                    halve(a, "max", 1)
+                    halve(a, "sum", 1)

@@ -19,6 +19,7 @@ NODES_PER_PARTITION = NODES // P
 HALVES = H // P
 GATES = 4
 F_GATE, I_GATE, O_GATE, U_GATE = 0, 1, 2, 3
+GATE_ORDER = (I_GATE, U_GATE, F_GATE, O_GATE)
 WIDTHS = [1, 1] + [2] * (NODES_PER_PARTITION // 2 - 2) + [1, 1]
 ROUNDS = len(WIDTHS)
 STARTS = [sum(WIDTHS[:g]) for g in range(ROUNDS)]
@@ -52,19 +53,23 @@ def tile_treelstmcellv2_kernel(
         loads = ctx.enter_context(tc.tile_pool(name="loads", bufs=AHEAD + 2))
         work = ctx.enter_context(tc.tile_pool(name="work", bufs=2))
         psum_one = ctx.enter_context(tc.psum_pool(name="psum_one", bufs=1))
-        psum_gate = ctx.enter_context(tc.psum_pool(name="psum_gate", bufs=GATES))
+        psum_two = ctx.enter_context(tc.psum_pool(name="psum_two", bufs=2))
+        psum_gate = ctx.enter_context(tc.psum_pool(name="psum_gate", bufs=GATES - 1))
 
         h_tiles, c_tiles = {}, {}
 
-        def load(g):
-            rows = slice(STARTS[g], STARTS[g] + WIDTHS[g])
+        def load_h(g):
             h_sb = loads.tile([P, WIDTHS[g], KIDS, H], BF16)
-            nc.sync.dma_start(out=h_sb[:], in_=h_rows[:, rows])
-            c_sb = loads.tile([P, WIDTHS[g], BLOCKS, H], BF16)
-            nc.sync.dma_start(out=c_sb[:], in_=c_rows[:, rows])
-            h_tiles[g], c_tiles[g] = h_sb, c_sb
+            nc.sync.dma_start(out=h_sb[:], in_=h_rows[:, STARTS[g] : STARTS[g] + WIDTHS[g]])
+            h_tiles[g] = h_sb
 
-        load(0)
+        def load_c(g):
+            c_sb = loads.tile([P, WIDTHS[g], BLOCKS, H], BF16)
+            nc.sync.dma_start(out=c_sb[:], in_=c_rows[:, STARTS[g] : STARTS[g] + WIDTHS[g]])
+            c_tiles[g] = c_sb
+
+        for g in range(AHEAD):
+            load_h(g)
 
         ident_f32 = keep.tile([P, P], F32)
         make_identity(nc, ident_f32[:])
@@ -113,12 +118,12 @@ def tile_treelstmcellv2_kernel(
         bias_cols = keep.tile([P, GATES * HALVES], F32)
         nc.vector.tensor_copy(out=bias_cols[:], in_=bias_ps[:, 0 : GATES * HALVES])
 
-        for g in range(1, AHEAD):
-            load(g)
+        for g in range(AHEAD - 1):
+            load_c(g)
 
         tree_tiles, hc_tiles, hcT_banks, hcT_tiles, hq_tiles = {}, {}, {}, {}, {}
         csT_banks = {}
-        gate_banks, gate_tiles, prod_tiles, back_banks, out_tiles = {}, {}, {}, {}, {}
+        gate_tiles, prod_tiles, back_banks, out_tiles = {}, {}, {}, {}
 
         trees = {"sum": (ALU.add, F32, 0), "max": (ALU.max, BF16, H)}
 
@@ -162,7 +167,7 @@ def tile_treelstmcellv2_kernel(
 
         def sum_c(g):
             c_sb = c_tiles[g]
-            csT_ps = psum_one.tile([P, HALVES, WIDTHS[g] * P], F32)
+            csT_ps = psum_two.tile([P, HALVES, WIDTHS[g] * P], F32)
             for half in range(HALVES):
                 for j in range(WIDTHS[g]):
                     for q in range(BLOCKS):
@@ -176,10 +181,11 @@ def tile_treelstmcellv2_kernel(
                         )
             csT_banks[g] = csT_ps
 
-        def gate_products(g):
+        def gates(g):
             hq_words, hq_scales = hq_tiles[g]
-            banks = []
-            for gate in range(GATES):
+            banks, acts = {}, {}
+
+            def passes(gate):
                 gate_ps = psum_gate.tile([P, HALVES, WIDTHS[g] * P], F32)
                 for half in range(HALVES):
                     cols = slice((gate * HALVES + half) * P, (gate * HALVES + half + 1) * P)
@@ -192,23 +198,27 @@ def tile_treelstmcellv2_kernel(
                         start=True,
                         stop=True,
                     )
-                banks.append(gate_ps)
-            gate_banks[g] = banks
+                banks[gate] = gate_ps
 
-        def gate_activations(g):
-            acts = {}
-            for gate in (I_GATE, U_GATE, F_GATE, O_GATE):
+            def activate(gate):
                 gate_sb = work.tile([P, HALVES, WIDTHS[g] * P], F32, name="gate_sb_%d" % gate)
                 for half in range(HALVES):
                     column = gate * HALVES + half
                     nc.scalar.activation(
                         out=gate_sb[:, half, :],
-                        in_=gate_banks[g][gate][:, half, :],
+                        in_=banks[gate][:, half, :],
                         func=ACT.Tanh if gate == U_GATE else ACT.Sigmoid,
                         bias=bias_cols[:, column : column + 1],
                         scale=1.0,
                     )
                 acts[gate] = gate_sb
+
+            for gate in GATE_ORDER[: GATES - 1]:
+                passes(gate)
+            activate(GATE_ORDER[0])
+            passes(GATE_ORDER[GATES - 1])
+            for gate in GATE_ORDER[1:]:
+                activate(gate)
             gate_tiles[g] = acts
 
         def multiply(g):
@@ -260,7 +270,9 @@ def tile_treelstmcellv2_kernel(
             for step in range(ROUNDS + 3):
                 a, b, c, d = step, step - 1, step - 2, step - 3
                 if live(a + AHEAD):
-                    load(a + AHEAD)
+                    load_h(a + AHEAD)
+                if live(a + AHEAD - 1):
+                    load_c(a + AHEAD - 1)
                 if live(d):
                     finish_h(d)
                 if live(c):
@@ -277,9 +289,9 @@ def tile_treelstmcellv2_kernel(
                     transpose_back(c)
                     finish_c(c)
                 if live(b):
-                    sum_c(b)
-                    gate_products(b)
-                    gate_activations(b)
+                    gates(b)
+                if live(a):
+                    sum_c(a)
                 if live(a):
                     halve(a, "max", 2)
                     halve(a, "sum", 2)

@@ -15,18 +15,17 @@ ALU = mybir.AluOpType
 NODES, KIDS, H = 2048, 8, 256
 P = 128
 PACK = 4
-NODES_PER_PARTITION = NODES // P
+LOTS = NODES // P
 HALVES = H // P
 GATES = 4
 F_GATE, I_GATE, O_GATE, U_GATE = 0, 1, 2, 3
 GATE_ORDER = (I_GATE, U_GATE, F_GATE, O_GATE)
-WIDTHS = [1, 1] + [2] * (NODES_PER_PARTITION // 2 - 2) + [1, 1]
-ROUNDS = len(WIDTHS)
-STARTS = [sum(WIDTHS[:g]) for g in range(ROUNDS)]
-assert sum(WIDTHS) == NODES_PER_PARTITION
-AHEAD = 2
 NODES_PER_BLOCK = P // KIDS
 BLOCKS = P // NODES_PER_BLOCK
+WIDTHS = [1] + [2] * (LOTS // 2 - 1) + [1]
+ROUNDS = len(WIDTHS)
+STARTS = [sum(WIDTHS[:g]) for g in range(ROUNDS)]
+AHEAD = 2
 
 FLOPS = 2 * NODES * (2 * H) * (GATES * H)
 
@@ -76,7 +75,7 @@ def tile_treelstmcellv2_kernel(
         ident_bf16 = keep.tile([P, P], BF16)
         make_identity(nc, ident_bf16[:])
         add_kids = keep.tile([P, NODES_PER_BLOCK], BF16)
-        with nc.allow_low_precision(reason="sums of one 1 and seven 0s are exact"):
+        with nc.allow_low_precision(reason="a sum of one 1 and seven 0s is exact"):
             nc.vector.tensor_reduce(
                 out=add_kids[:],
                 in_=ident_bf16[:].rearrange("p (n k) -> p n k", k=KIDS),
@@ -98,13 +97,13 @@ def tile_treelstmcellv2_kernel(
         f_scale_rows = U_f_w_scales.rearrange("g q n -> (g q) n")
         iou_scale_rows = U_iou_w_scales.rearrange("g q n -> (g q) n")
         for quadrant in range(4):
-            live_rows = slice(32 * quadrant, 32 * quadrant + 4)
+            partitions = slice(32 * quadrant, 32 * quadrant + 4)
             rows = slice(4 * quadrant, 4 * quadrant + 4)
             nc.sync.dma_start(
-                out=w_scales[live_rows, 0:H].bitcast(I32), in_=f_scale_rows[rows, :].bitcast(I32)
+                out=w_scales[partitions, 0:H].bitcast(I32), in_=f_scale_rows[rows, :].bitcast(I32)
             )
             nc.sync.dma_start(
-                out=w_scales[live_rows, H : GATES * H].bitcast(I32), in_=iou_scale_rows[rows, :].bitcast(I32)
+                out=w_scales[partitions, H : GATES * H].bitcast(I32), in_=iou_scale_rows[rows, :].bitcast(I32)
             )
 
         bias_rows = keep.tile([P, P], BF16)
@@ -121,9 +120,8 @@ def tile_treelstmcellv2_kernel(
         for g in range(AHEAD - 1):
             load_c(g)
 
-        tree_tiles, hc_tiles, hcT_banks, hcT_tiles, hq_tiles = {}, {}, {}, {}, {}
-        csT_banks = {}
-        gate_tiles, prod_tiles, back_banks, out_tiles = {}, {}, {}, {}
+        tree_tiles, hc_tiles, hcT_banks, hcT_tiles, hq_tiles, csT_banks = {}, {}, {}, {}, {}, {}
+        gate_tiles, product_tiles, back_banks, out_tiles = {}, {}, {}, {}
 
         trees = {"sum": (ALU.add, F32, 0), "max": (ALU.max, BF16, H)}
 
@@ -151,9 +149,9 @@ def tile_treelstmcellv2_kernel(
             hcT_banks[g] = hcT_ps
 
         def regroup_hc(g):
-            hcT = work.tile([P, WIDTHS[g], P, PACK], BF16, align_bytes=64)
-            nc.scalar.copy(out=hcT[:], in_=hcT_banks[g][:].rearrange("p j t r -> p j r t"))
-            hcT_tiles[g] = hcT
+            hcT_sb = work.tile([P, WIDTHS[g], P, PACK], BF16, align_bytes=64)
+            nc.scalar.copy(out=hcT_sb[:], in_=hcT_banks[g][:].rearrange("p j t r -> p j r t"))
+            hcT_tiles[g] = hcT_sb
 
         def quantise_hc(g):
             hq_words = work.tile([P, WIDTHS[g] * P], U32, align_bytes=64)
@@ -227,10 +225,10 @@ def tile_treelstmcellv2_kernel(
             nc.vector.tensor_tensor(out=iu[:], in0=acts[I_GATE][:], in1=acts[U_GATE][:], op=ALU.mult)
             fc = work.tile([P, HALVES, WIDTHS[g] * P], F32)
             nc.vector.tensor_tensor(out=fc[:], in0=acts[F_GATE][:], in1=csT_banks[g][:], op=ALU.mult)
-            prod_tiles[g] = (iu, fc)
+            product_tiles[g] = (iu, fc)
 
         def transpose_back(g):
-            iu, fc = prod_tiles[g]
+            iu, fc = product_tiles[g]
             o_sb = gate_tiles[g][O_GATE]
             c_ps = psum_one.tile([P, WIDTHS[g], H], F32)
             o_ps = psum_one.tile([P, WIDTHS[g], H], F32)
@@ -268,32 +266,31 @@ def tile_treelstmcellv2_kernel(
 
         with tc.manual_schedule():
             for step in range(ROUNDS + 3):
-                a, b, c, d = step, step - 1, step - 2, step - 3
-                if live(a + AHEAD):
-                    load_h(a + AHEAD)
-                if live(a + AHEAD - 1):
-                    load_c(a + AHEAD - 1)
-                if live(d):
-                    finish_h(d)
-                if live(c):
-                    multiply(c)
-                if live(b):
-                    transpose_hc(b)
-                    regroup_hc(b)
-                if live(a):
-                    halve(a, "max", 4)
-                    halve(a, "sum", 4)
-                if live(b):
-                    quantise_hc(b)
-                if live(c):
-                    transpose_back(c)
-                    finish_c(c)
-                if live(b):
-                    gates(b)
-                if live(a):
-                    sum_c(a)
-                if live(a):
-                    halve(a, "max", 2)
-                    halve(a, "sum", 2)
-                    halve(a, "max", 1)
-                    halve(a, "sum", 1)
+                r1, r2, r3, r4 = step, step - 1, step - 2, step - 3
+                if live(r1 + AHEAD):
+                    load_h(r1 + AHEAD)
+                if live(r1 + AHEAD - 1):
+                    load_c(r1 + AHEAD - 1)
+                if live(r4):
+                    finish_h(r4)
+                if live(r3):
+                    multiply(r3)
+                if live(r2):
+                    transpose_hc(r2)
+                    regroup_hc(r2)
+                if live(r1):
+                    halve(r1, "max", 4)
+                    halve(r1, "sum", 4)
+                if live(r2):
+                    quantise_hc(r2)
+                if live(r3):
+                    transpose_back(r3)
+                    finish_c(r3)
+                if live(r2):
+                    gates(r2)
+                if live(r1):
+                    sum_c(r1)
+                    halve(r1, "max", 2)
+                    halve(r1, "sum", 2)
+                    halve(r1, "max", 1)
+                    halve(r1, "sum", 1)

@@ -20,6 +20,8 @@ HALVES = H // P
 GATES = 4
 F_GATE, I_GATE, O_GATE, U_GATE = 0, 1, 2, 3
 GATE_ORDER = (I_GATE, U_GATE, F_GATE, O_GATE)
+PARTS = KIDS // 2
+QUARTER = H // PACK
 NODES_PER_BLOCK = P // KIDS
 BLOCKS = P // NODES_PER_BLOCK
 WIDTHS = [1] + [2] * (LOTS // 2 - 1) + [1]
@@ -112,45 +114,61 @@ def tile_treelstmcellv2_kernel(
         nc.sync.dma_start(
             out=bias_rows[HALVES : GATES * HALVES, :], in_=b_iou.rearrange("o (j m) -> (o j) m", m=P)
         )
-        bias_ps = psum_one.tile([P, P], BF16, tag="hcT_ps")
+        bias_ps = psum_one.tile([P, P], BF16, tag="csT_ps")
         nc.tensor.transpose(bias_ps[:], bias_rows[:], ident_bf16[:])
         bias_cols = keep.tile([P, GATES * HALVES], F32)
         nc.vector.tensor_copy(out=bias_cols[:], in_=bias_ps[:, 0 : GATES * HALVES])
 
+        parts_tiles = []
+        for parity in range(2):
+            parts = keep.tile([P, 2, PARTS, PACK, P], F32, name="parts_%d" % parity)
+            engine = nc.vector if parity == 0 else nc.gpsimd
+            for j in range(2):
+                engine.memset(parts[:, j, 1:PARTS, :, QUARTER:P], 0.0)
+            parts_tiles.append(parts)
+
         for g in range(AHEAD - 1):
             load_c(g)
 
-        tree_tiles, hc_tiles, hcT_banks, hcT_tiles, hq_tiles, csT_banks = {}, {}, {}, {}, {}, {}
+        tree_tiles, hcT_banks, hcT_tiles, hq_tiles, csT_banks = {}, {}, {}, {}, {}
         gate_tiles, product_tiles, back_banks, out_tiles = {}, {}, {}, {}
 
-        trees = {"sum": (ALU.add, F32, 0), "max": (ALU.max, BF16, H)}
-
-        def halve(g, tree, kids):
-            op, dtype, column = trees[tree]
-            src = tree_tiles.get((g, tree), h_tiles[g])
+        def max_level(g, kids):
+            src = tree_tiles.get(g, h_tiles[g])
+            in0, in1 = src[:, :, 0:kids, :], src[:, :, kids : 2 * kids, :]
             if kids > 1:
-                dst = work.tile([P, WIDTHS[g], kids, H], dtype, name="%s_%d" % (tree, kids))
-                nc.vector.tensor_tensor(out=dst[:], in0=src[:, :, 0:kids, :], in1=src[:, :, kids : 2 * kids, :], op=op)
-                tree_tiles[(g, tree)] = dst
+                dst = work.tile([P, WIDTHS[g], kids, H], BF16, name="max_%d" % kids)
+                nc.vector.tensor_tensor(out=dst[:], in0=in0, in1=in1, op=ALU.max)
+                tree_tiles[g] = dst
             else:
-                if g not in hc_tiles:
-                    hc = work.tile([P, WIDTHS[g], 2 * H], BF16)
-                    hc_tiles[g] = hc
                 nc.vector.tensor_tensor(
-                    out=hc_tiles[g][:, :, column : column + H], in0=src[:, :, 0, :], in1=src[:, :, 1, :], op=op
+                    out=parts_tiles[g % 2][:, 0 : WIDTHS[g], 0, :, QUARTER:P],
+                    in0=src[:, :, 0, :].rearrange("p l (f t) -> p l t f", t=PACK),
+                    in1=src[:, :, 1, :].rearrange("p l (f t) -> p l t f", t=PACK),
+                    op=ALU.max,
                 )
 
+        def add_pairs(g, j):
+            pairs = h_tiles[g][:, j].rearrange("p (k two) (f t) -> p two k t f", two=2, t=PACK)
+            nc.vector.tensor_tensor(
+                out=parts_tiles[g % 2][:, j, :, :, 0:QUARTER], in0=pairs[:, 0], in1=pairs[:, 1], op=ALU.add
+            )
+
         def transpose_hc(g):
-            hc = hc_tiles[g]
-            hcT_ps = psum_one.tile([P, WIDTHS[g], PACK, P], BF16)
             for j in range(WIDTHS[g]):
+                hcT_ps = psum_two.tile([P, PACK, P], F32)
                 for t in range(PACK):
-                    nc.tensor.transpose(hcT_ps[:, j, t, :], hc[:, j, t : 2 * H : PACK], ident_bf16[:])
-            hcT_banks[g] = hcT_ps
+                    for part in range(PARTS):
+                        nc.tensor.matmul(
+                            out=hcT_ps[:, t, :], lhsT=parts_tiles[g % 2][:, j, part, t, :], rhs=ident_f32[:],
+                            is_transpose=True, start=(part == 0), stop=(part == PARTS - 1),
+                        )
+                hcT_banks[(g, j)] = hcT_ps
 
         def regroup_hc(g):
             hcT_sb = work.tile([P, WIDTHS[g], P, PACK], BF16, align_bytes=64)
-            nc.scalar.copy(out=hcT_sb[:], in_=hcT_banks[g][:].rearrange("p j t r -> p j r t"))
+            for j in range(WIDTHS[g]):
+                nc.scalar.copy(out=hcT_sb[:, j], in_=hcT_banks[(g, j)][:].rearrange("p t r -> p r t"))
             hcT_tiles[g] = hcT_sb
 
         def quantise_hc(g):
@@ -165,7 +183,7 @@ def tile_treelstmcellv2_kernel(
 
         def sum_c(g):
             c_sb = c_tiles[g]
-            csT_ps = psum_two.tile([P, HALVES, WIDTHS[g] * P], F32)
+            csT_ps = psum_one.tile([P, HALVES, WIDTHS[g] * P], F32)
             for half in range(HALVES):
                 for j in range(WIDTHS[g]):
                     for q in range(BLOCKS):
@@ -219,13 +237,17 @@ def tile_treelstmcellv2_kernel(
                 activate(gate)
             gate_tiles[g] = acts
 
-        def multiply(g):
+        def multiply_iu(g):
             acts = gate_tiles[g]
             iu = work.tile([P, HALVES, WIDTHS[g] * P], F32)
             nc.vector.tensor_tensor(out=iu[:], in0=acts[I_GATE][:], in1=acts[U_GATE][:], op=ALU.mult)
+            product_tiles[g] = iu
+
+        def multiply_fc(g):
+            acts = gate_tiles[g]
             fc = work.tile([P, HALVES, WIDTHS[g] * P], F32)
             nc.vector.tensor_tensor(out=fc[:], in0=acts[F_GATE][:], in1=csT_banks[g][:], op=ALU.mult)
-            product_tiles[g] = (iu, fc)
+            product_tiles[g] = (product_tiles[g], fc)
 
         def transpose_back(g):
             iu, fc = product_tiles[g]
@@ -273,24 +295,28 @@ def tile_treelstmcellv2_kernel(
                     load_c(r1 + AHEAD - 1)
                 if live(r4):
                     finish_h(r4)
-                if live(r3):
-                    multiply(r3)
                 if live(r2):
                     transpose_hc(r2)
                     regroup_hc(r2)
                 if live(r1):
-                    halve(r1, "max", 4)
-                    halve(r1, "sum", 4)
+                    max_level(r1, 4)
+                if live(r3):
+                    multiply_iu(r3)
+                if live(r1):
+                    max_level(r1, 2)
+                if live(r3):
+                    multiply_fc(r3)
+                if live(r1):
+                    max_level(r1, 1)
+                    add_pairs(r1, 0)
                 if live(r2):
                     quantise_hc(r2)
                 if live(r3):
                     transpose_back(r3)
                     finish_c(r3)
                 if live(r2):
+                    sum_c(r2)
                     gates(r2)
                 if live(r1):
-                    sum_c(r1)
-                    halve(r1, "max", 2)
-                    halve(r1, "sum", 2)
-                    halve(r1, "max", 1)
-                    halve(r1, "sum", 1)
+                    for j in range(1, WIDTHS[r1]):
+                        add_pairs(r1, j)

@@ -52,7 +52,8 @@ def tile_treelstmcellv2_kernel(
     with ExitStack() as ctx:
         keep = ctx.enter_context(tc.tile_pool(name="keep", bufs=1))
         loads = ctx.enter_context(tc.tile_pool(name="loads", bufs=AHEAD + 2))
-        work = ctx.enter_context(tc.tile_pool(name="work", bufs=2))
+        work = ctx.enter_context(tc.tile_pool(name="work", bufs=3))
+        stores = ctx.enter_context(tc.tile_pool(name="stores", bufs=4))
         psum_one = ctx.enter_context(tc.psum_pool(name="psum_one", bufs=1))
         psum_two = ctx.enter_context(tc.psum_pool(name="psum_two", bufs=2))
         psum_gate = ctx.enter_context(tc.psum_pool(name="psum_gate", bufs=GATES - 1))
@@ -271,7 +272,7 @@ def tile_treelstmcellv2_kernel(
 
         def finish_c(g):
             c_ps, o_ps = back_banks[g]
-            out_sb = work.tile([P, WIDTHS[g], 2 * H], F32)
+            out_sb = stores.tile([P, WIDTHS[g], 2 * H], F32)
             nc.scalar.copy(out=out_sb[:, :, H : 2 * H], in_=c_ps[:])
             tanh_c = work.tile([P, WIDTHS[g], H], F32)
             nc.scalar.activation(out=tanh_c[:], in_=c_ps[:], func=ACT.Tanh)

@@ -26,6 +26,7 @@ NODES_PER_BLOCK = P // KIDS
 BLOCKS = P // NODES_PER_BLOCK
 WIDTHS = [1] + [2] * (LOTS // 2 - 1) + [1]
 ROUNDS = len(WIDTHS)
+V_COPIES = ROUNDS - 3
 STARTS = [sum(WIDTHS[:g]) for g in range(ROUNDS)]
 AHEAD = 2
 
@@ -45,9 +46,9 @@ def tile_treelstmcellv2_kernel(
     out,
 ):
     nc = tc.nc
-    h_rows = mailbox_h.rearrange("(t p) k h -> p t k h", p=P)
-    c_rows = mailbox_c.rearrange("(t q n) k h -> (n k) t q h", q=BLOCKS, n=NODES_PER_BLOCK)
-    out_rows = out.rearrange("(t p) f -> p t f", p=P)
+
+    def nodes_of(g, array):
+        return array[STARTS[g] * P : (STARTS[g] + WIDTHS[g]) * P]
 
     with ExitStack() as ctx:
         keep = ctx.enter_context(tc.tile_pool(name="keep", bufs=1))
@@ -62,12 +63,12 @@ def tile_treelstmcellv2_kernel(
 
         def load_h(g):
             h_sb = loads.tile([P, WIDTHS[g], KIDS, H], BF16)
-            nc.sync.dma_start(out=h_sb[:], in_=h_rows[:, STARTS[g] : STARTS[g] + WIDTHS[g]])
+            nc.sync.dma_start(out=h_sb[:], in_=nodes_of(g, mailbox_h).rearrange("(p l) k h -> p l k h", l=WIDTHS[g]))
             h_tiles[g] = h_sb
 
         def load_c(g):
-            c_sb = loads.tile([P, WIDTHS[g], BLOCKS, H], BF16)
-            nc.sync.dma_start(out=c_sb[:], in_=c_rows[:, STARTS[g] : STARTS[g] + WIDTHS[g]])
+            c_sb = loads.tile([P, WIDTHS[g] * BLOCKS, H], BF16)
+            nc.sync.dma_start(out=c_sb[:], in_=nodes_of(g, mailbox_c).rearrange("(q n) k h -> (n k) q h", n=NODES_PER_BLOCK))
             c_tiles[g] = c_sb
 
         for g in range(AHEAD):
@@ -111,8 +112,8 @@ def tile_treelstmcellv2_kernel(
 
         bias_rows = keep.tile([P, P], BF16)
         nc.vector.memset(bias_rows[:], 0.0)
-        nc.sync.dma_start(out=bias_rows[0:HALVES, :], in_=U_f_b.rearrange("(j m) -> j m", m=P))
-        nc.sync.dma_start(
+        nc.gpsimd.dma_start(out=bias_rows[0:HALVES, :], in_=U_f_b.rearrange("(j m) -> j m", m=P))
+        nc.gpsimd.dma_start(
             out=bias_rows[HALVES : GATES * HALVES, :], in_=b_iou.rearrange("o (j m) -> (o j) m", m=P)
         )
         bias_ps = psum_one.tile([P, P], BF16, tag="csT_ps")
@@ -186,16 +187,15 @@ def tile_treelstmcellv2_kernel(
             c_sb = c_tiles[g]
             csT_ps = psum_one.tile([P, HALVES, WIDTHS[g] * P], F32)
             for half in range(HALVES):
-                for j in range(WIDTHS[g]):
-                    for q in range(BLOCKS):
-                        first = j * P + q * NODES_PER_BLOCK
-                        nc.tensor.matmul(
-                            out=csT_ps[:, half, first : first + NODES_PER_BLOCK],
-                            lhsT=c_sb[:, j, q, half * P : (half + 1) * P],
-                            rhs=add_kids[:],
-                            start=True,
-                            stop=True,
-                        )
+                for q in range(WIDTHS[g] * BLOCKS):
+                    first = q * NODES_PER_BLOCK
+                    nc.tensor.matmul(
+                        out=csT_ps[:, half, first : first + NODES_PER_BLOCK],
+                        lhsT=c_sb[:, q, half * P : (half + 1) * P],
+                        rhs=add_kids[:],
+                        start=True,
+                        stop=True,
+                    )
             csT_banks[g] = csT_ps
 
         def gates(g):
@@ -247,7 +247,13 @@ def tile_treelstmcellv2_kernel(
         def multiply_fc(g):
             acts = gate_tiles[g]
             fc = work.tile([P, HALVES, WIDTHS[g] * P], F32)
-            nc.vector.tensor_tensor(out=fc[:], in0=acts[F_GATE][:], in1=csT_banks[g][:], op=ALU.mult)
+            lots = "p h (l r) -> p h l r"
+            nc.vector.tensor_tensor(
+                out=fc[:].rearrange(lots, r=P),
+                in0=acts[F_GATE][:].rearrange(lots, r=P),
+                in1=csT_banks[g][:].rearrange("p h (r l) -> p h l r", r=P),
+                op=ALU.mult,
+            )
             product_tiles[g] = (product_tiles[g], fc)
 
         def transpose_back(g):
@@ -273,16 +279,19 @@ def tile_treelstmcellv2_kernel(
         def finish_c(g):
             c_ps, o_ps = back_banks[g]
             out_sb = stores.tile([P, WIDTHS[g], 2 * H], F32)
-            nc.scalar.copy(out=out_sb[:, :, H : 2 * H], in_=c_ps[:])
             tanh_c = work.tile([P, WIDTHS[g], H], F32)
             nc.scalar.activation(out=tanh_c[:], in_=c_ps[:], func=ACT.Tanh)
+            if g < V_COPIES:
+                nc.scalar.copy(out=out_sb[:, :, H : 2 * H], in_=c_ps[:])
+            else:
+                nc.vector.tensor_copy(out=out_sb[:, :, H : 2 * H], in_=c_ps[:])
             out_tiles[g] = (out_sb, tanh_c)
 
         def finish_h(g):
             c_ps, o_ps = back_banks[g]
             out_sb, tanh_c = out_tiles[g]
             nc.vector.tensor_tensor(out=out_sb[:, :, 0:H], in0=o_ps[:], in1=tanh_c[:], op=ALU.mult)
-            nc.sync.dma_start(out=out_rows[:, STARTS[g] : STARTS[g] + WIDTHS[g]], in_=out_sb[:])
+            nc.sync.dma_start(out=nodes_of(g, out).rearrange("(p l) f -> p l f", l=WIDTHS[g]), in_=out_sb[:])
 
         def live(g):
             return 0 <= g < ROUNDS

@@ -203,7 +203,8 @@ def tile_treelstmcellv2_kernel(
             banks, acts = {}, {}
 
             def passes(gate):
-                gate_ps = psum_gate.tile([P, HALVES, WIDTHS[g] * P], F32)
+                pool, tag = (psum_two, "hcT_ps") if gate == I_GATE else (psum_gate, "gate_ps")
+                gate_ps = pool.tile([P, HALVES, WIDTHS[g] * P], F32, tag=tag)
                 for half in range(HALVES):
                     cols = slice((gate * HALVES + half) * P, (gate * HALVES + half + 1) * P)
                     nc.tensor.matmul_mx(
@@ -230,18 +231,19 @@ def tile_treelstmcellv2_kernel(
                     )
                 acts[gate] = gate_sb
 
-            for gate in GATE_ORDER[: GATES - 1]:
+            for gate in GATE_ORDER:
                 passes(gate)
-            activate(GATE_ORDER[0])
-            passes(GATE_ORDER[GATES - 1])
-            for gate in GATE_ORDER[1:]:
+            for gate in GATE_ORDER:
                 activate(gate)
             gate_tiles[g] = acts
 
-        def multiply_iu(g):
+        def multiply_iu(g, newest):
             acts = gate_tiles[g]
+            if newest is not None:
+                held = work.tile([P, 1], F32)
+                nc.gpsimd.tensor_copy(out=held[:], in_=newest)
             iu = work.tile([P, HALVES, WIDTHS[g] * P], F32)
-            nc.vector.tensor_tensor(out=iu[:], in0=acts[I_GATE][:], in1=acts[U_GATE][:], op=ALU.mult)
+            nc.gpsimd.tensor_tensor(out=iu[:], in0=acts[I_GATE][:], in1=acts[U_GATE][:], op=ALU.mult)
             product_tiles[g] = iu
 
         def multiply_fc(g):
@@ -303,30 +305,33 @@ def tile_treelstmcellv2_kernel(
                     load_h(r1 + AHEAD)
                 if live(r1 + AHEAD - 1):
                     load_c(r1 + AHEAD - 1)
-                if live(r4):
-                    finish_h(r4)
-                if live(r2):
-                    transpose_hc(r2)
-                    regroup_hc(r2)
                 if live(r1):
                     max_level(r1, 4)
+                if live(r4):
+                    finish_h(r4)
                 if live(r3):
-                    multiply_iu(r3)
-                if live(r1):
-                    max_level(r1, 2)
+                    multiply_iu(r3, parts_tiles[r2 % 2][:, WIDTHS[r2] - 1, 0, PACK - 1, P - 1 : P] if live(r2) else None)
                 if live(r3):
                     multiply_fc(r3)
+                if live(r2):
+                    transpose_hc(r2)
+                if live(r2):
+                    regroup_hc(r2)
                 if live(r1):
-                    max_level(r1, 1)
                     add_pairs(r1, 0)
+                if live(r1):
+                    max_level(r1, 2)
                 if live(r2):
                     quantise_hc(r2)
+                if live(r1) and WIDTHS[r1] > 1:
+                    add_pairs(r1, 1)
                 if live(r3):
                     transpose_back(r3)
+                if live(r3):
                     finish_c(r3)
                 if live(r2):
                     sum_c(r2)
+                if live(r2):
                     gates(r2)
                 if live(r1):
-                    for j in range(1, WIDTHS[r1]):
-                        add_pairs(r1, j)
+                    max_level(r1, 1)

from contextlib import ExitStack

import concourse.mybir as mybir
from concourse.masks import make_identity

F32 = mybir.dt.float32
BF16 = mybir.dt.bfloat16
I32 = mybir.dt.int32
U32 = mybir.dt.uint32
U8 = mybir.dt.uint8
FP8X4 = mybir.dt.float8_e4m3fn_x4
ACT = mybir.ActivationFunctionType
ALU = mybir.AluOpType

NODES, KIDS, H = 2048, 8, 256
P = 128
PACK = 4
LOTS = NODES // P
HALVES = H // P
GATES = 4
F_GATE, I_GATE, O_GATE, U_GATE = 0, 1, 2, 3
GATE_ORDER = (I_GATE, U_GATE, F_GATE, O_GATE)
PARTS = KIDS // 2
QUARTER = H // PACK
NODES_PER_BLOCK = P // KIDS
BLOCKS = P // NODES_PER_BLOCK
WIDTHS = [1] + [2] * (LOTS // 2 - 1) + [1]
ROUNDS = len(WIDTHS)
V_COPIES = ROUNDS - 3
STARTS = [sum(WIDTHS[:g]) for g in range(ROUNDS)]
AHEAD = 2

FLOPS = 2 * NODES * (2 * H) * (GATES * H)


def tile_treelstmcellv2_kernel(
    tc,
    mailbox_h,
    mailbox_c,
    U_iou_w_words,
    U_iou_w_scales,
    b_iou,
    U_f_w_words,
    U_f_w_scales,
    U_f_b,
    out,
):
    nc = tc.nc

    def nodes_of(g, array):
        return array[STARTS[g] * P : (STARTS[g] + WIDTHS[g]) * P]

    with ExitStack() as ctx:
        keep = ctx.enter_context(tc.tile_pool(name="keep", bufs=1))
        loads = ctx.enter_context(tc.tile_pool(name="loads", bufs=AHEAD + 2))
        work = ctx.enter_context(tc.tile_pool(name="work", bufs=3))
        stores = ctx.enter_context(tc.tile_pool(name="stores", bufs=4))
        psum_one = ctx.enter_context(tc.psum_pool(name="psum_one", bufs=1))
        psum_two = ctx.enter_context(tc.psum_pool(name="psum_two", bufs=2))
        psum_gate = ctx.enter_context(tc.psum_pool(name="psum_gate", bufs=GATES - 1))

        h_tiles, c_tiles = {}, {}

        def load_h(g):
            h_sb = loads.tile([P, WIDTHS[g], KIDS, H], BF16)
            nc.sync.dma_start(out=h_sb[:], in_=nodes_of(g, mailbox_h).rearrange("(p l) k h -> p l k h", l=WIDTHS[g]))
            h_tiles[g] = h_sb

        def load_c(g):
            c_sb = loads.tile([P, WIDTHS[g] * BLOCKS, H], BF16)
            nc.sync.dma_start(out=c_sb[:], in_=nodes_of(g, mailbox_c).rearrange("(q n) k h -> (n k) q h", n=NODES_PER_BLOCK))
            c_tiles[g] = c_sb

        for g in range(AHEAD):
            load_h(g)

        ident_f32 = keep.tile([P, P], F32)
        make_identity(nc, ident_f32[:])
        ident_bf16 = keep.tile([P, P], BF16)
        make_identity(nc, ident_bf16[:])
        add_kids = keep.tile([P, NODES_PER_BLOCK], BF16)
        with nc.allow_low_precision(reason="a sum of one 1 and seven 0s is exact"):
            nc.vector.tensor_reduce(
                out=add_kids[:],
                in_=ident_bf16[:].rearrange("p (n k) -> p n k", k=KIDS),
                axis=mybir.AxisListType.X,
                op=ALU.add,
            )

        w_words = keep.tile([P, GATES * H], U32, align_bytes=64)
        nc.sync.dma_start(
            out=w_words[:, 0:H].bitcast(I32),
            in_=U_f_w_words.rearrange("g p n t -> (g p) (n t)").bitcast(I32),
        )
        nc.sync.dma_start(
            out=w_words[:, H : GATES * H].bitcast(I32),
            in_=U_iou_w_words.rearrange("g p n t -> (g p) (n t)").bitcast(I32),
        )
        w_scales = keep.tile([P, GATES * H], U8, align_bytes=64)
        nc.vector.memset(w_scales[:].bitcast(I32), 0)
        f_scale_rows = U_f_w_scales.rearrange("g q n -> (g q) n")
        iou_scale_rows = U_iou_w_scales.rearrange("g q n -> (g q) n")
        for quadrant in range(4):
            partitions = slice(32 * quadrant, 32 * quadrant + 4)
            rows = slice(4 * quadrant, 4 * quadrant + 4)
            nc.sync.dma_start(
                out=w_scales[partitions, 0:H].bitcast(I32), in_=f_scale_rows[rows, :].bitcast(I32)
            )
            nc.sync.dma_start(
                out=w_scales[partitions, H : GATES * H].bitcast(I32), in_=iou_scale_rows[rows, :].bitcast(I32)
            )

        bias_rows = keep.tile([P, P], BF16)
        nc.vector.memset(bias_rows[:], 0.0)
        nc.gpsimd.dma_start(out=bias_rows[0:HALVES, :], in_=U_f_b.rearrange("(j m) -> j m", m=P))
        nc.gpsimd.dma_start(
            out=bias_rows[HALVES : GATES * HALVES, :], in_=b_iou.rearrange("o (j m) -> (o j) m", m=P)
        )
        bias_ps = psum_one.tile([P, P], BF16, tag="csT_ps")
        nc.tensor.transpose(bias_ps[:], bias_rows[:], ident_bf16[:])
        bias_cols = keep.tile([P, GATES * HALVES], F32)
        nc.vector.tensor_copy(out=bias_cols[:], in_=bias_ps[:, 0 : GATES * HALVES])

        parts_tiles = []
        for parity in range(2):
            parts = keep.tile([P, 2, PARTS, PACK, P], F32, name="parts_%d" % parity)
            engine = nc.vector if parity == 0 else nc.gpsimd
            for j in range(2):
                engine.memset(parts[:, j, 1:PARTS, :, QUARTER:P], 0.0)
            parts_tiles.append(parts)

        for g in range(AHEAD - 1):
            load_c(g)

        tree_tiles, hcT_banks, hcT_tiles, hq_tiles, csT_banks = {}, {}, {}, {}, {}
        gate_tiles, product_tiles, back_banks, out_tiles = {}, {}, {}, {}

        def max_level(g, kids):
            src = tree_tiles.get(g, h_tiles[g])
            in0, in1 = src[:, :, 0:kids, :], src[:, :, kids : 2 * kids, :]
            if kids > 1:
                dst = work.tile([P, WIDTHS[g], kids, H], BF16, name="max_%d" % kids)
                nc.vector.tensor_tensor(out=dst[:], in0=in0, in1=in1, op=ALU.max)
                tree_tiles[g] = dst
            else:
                nc.vector.tensor_tensor(
                    out=parts_tiles[g % 2][:, 0 : WIDTHS[g], 0, :, QUARTER:P],
                    in0=src[:, :, 0, :].rearrange("p l (f t) -> p l t f", t=PACK),
                    in1=src[:, :, 1, :].rearrange("p l (f t) -> p l t f", t=PACK),
                    op=ALU.max,
                )

        def add_pairs(g, j):
            pairs = h_tiles[g][:, j].rearrange("p (k two) (f t) -> p two k t f", two=2, t=PACK)
            nc.vector.tensor_tensor(
                out=parts_tiles[g % 2][:, j, :, :, 0:QUARTER], in0=pairs[:, 0], in1=pairs[:, 1], op=ALU.add
            )

        def transpose_hc(g):
            for j in range(WIDTHS[g]):
                hcT_ps = psum_two.tile([P, PACK, P], F32)
                for t in range(PACK):
                    for part in range(PARTS):
                        nc.tensor.matmul(
                            out=hcT_ps[:, t, :], lhsT=parts_tiles[g % 2][:, j, part, t, :], rhs=ident_f32[:],
                            is_transpose=True, start=(part == 0), stop=(part == PARTS - 1),
                        )
                hcT_banks[(g, j)] = hcT_ps

        def regroup_hc(g):
            hcT_sb = work.tile([P, WIDTHS[g], P, PACK], BF16, align_bytes=64)
            for j in range(WIDTHS[g]):
                nc.scalar.copy(out=hcT_sb[:, j], in_=hcT_banks[(g, j)][:].rearrange("p t r -> p r t"))
            hcT_tiles[g] = hcT_sb

        def quantise_hc(g):
            hq_words = work.tile([P, WIDTHS[g] * P], U32, align_bytes=64)
            hq_scales = work.tile([P, WIDTHS[g] * P], U8, align_bytes=64)
            nc.vector.quantize_mx(
                out=hq_words[:].bitcast(FP8X4),
                scales=hq_scales[:],
                in_=hcT_tiles[g][:].rearrange("p j r t -> p (j r t)"),
            )
            hq_tiles[g] = (hq_words, hq_scales)

        def sum_c(g):
            c_sb = c_tiles[g]
            csT_ps = psum_one.tile([P, HALVES, WIDTHS[g] * P], F32)
            for half in range(HALVES):
                for q in range(WIDTHS[g] * BLOCKS):
                    first = q * NODES_PER_BLOCK
                    nc.tensor.matmul(
                        out=csT_ps[:, half, first : first + NODES_PER_BLOCK],
                        lhsT=c_sb[:, q, half * P : (half + 1) * P],
                        rhs=add_kids[:],
                        start=True,
                        stop=True,
                    )
            csT_banks[g] = csT_ps

        def gates(g):
            hq_words, hq_scales = hq_tiles[g]
            banks, acts = {}, {}

            def passes(gate):
                pool, tag = (psum_two, "hcT_ps") if gate == I_GATE else (psum_gate, "gate_ps")
                gate_ps = pool.tile([P, HALVES, WIDTHS[g] * P], F32, tag=tag)
                for half in range(HALVES):
                    cols = slice((gate * HALVES + half) * P, (gate * HALVES + half + 1) * P)
                    nc.tensor.matmul_mx(
                        out=gate_ps[:, half, :],
                        lhsT=w_words[:, cols].bitcast(FP8X4),
                        lhsT_scale=w_scales[:, cols],
                        rhs=hq_words[:].bitcast(FP8X4),
                        rhs_scale=hq_scales[:],
                        start=True,
                        stop=True,
                    )
                banks[gate] = gate_ps

            def activate(gate):
                gate_sb = work.tile([P, HALVES, WIDTHS[g] * P], F32, name="gate_sb_%d" % gate)
                for half in range(HALVES):
                    column = gate * HALVES + half
                    nc.scalar.activation(
                        out=gate_sb[:, half, :],
                        in_=banks[gate][:, half, :],
                        func=ACT.Tanh if gate == U_GATE else ACT.Sigmoid,
                        bias=bias_cols[:, column : column + 1],
                        scale=1.0,
                    )
                acts[gate] = gate_sb

            for gate in GATE_ORDER:
                passes(gate)
            for gate in GATE_ORDER:
                activate(gate)
            gate_tiles[g] = acts

        def multiply_iu(g, newest):
            acts = gate_tiles[g]
            if newest is not None:
                held = work.tile([P, 1], F32)
                nc.gpsimd.tensor_copy(out=held[:], in_=newest)
            iu = work.tile([P, HALVES, WIDTHS[g] * P], F32)
            nc.gpsimd.tensor_tensor(out=iu[:], in0=acts[I_GATE][:], in1=acts[U_GATE][:], op=ALU.mult)
            product_tiles[g] = iu

        def multiply_fc(g):
            acts = gate_tiles[g]
            fc = work.tile([P, HALVES, WIDTHS[g] * P], F32)
            lots = "p h (l r) -> p h l r"
            nc.vector.tensor_tensor(
                out=fc[:].rearrange(lots, r=P),
                in0=acts[F_GATE][:].rearrange(lots, r=P),
                in1=csT_banks[g][:].rearrange("p h (r l) -> p h l r", r=P),
                op=ALU.mult,
            )
            product_tiles[g] = (product_tiles[g], fc)

        def transpose_back(g):
            iu, fc = product_tiles[g]
            o_sb = gate_tiles[g][O_GATE]
            c_ps = psum_one.tile([P, WIDTHS[g], H], F32)
            o_ps = psum_one.tile([P, WIDTHS[g], H], F32)
            for j in range(WIDTHS[g]):
                for half in range(HALVES):
                    nodes = slice(j * P, (j + 1) * P)
                    feats = slice(half * P, (half + 1) * P)
                    nc.tensor.matmul(
                        out=c_ps[:, j, feats], lhsT=iu[:, half, nodes], rhs=ident_f32[:],
                        is_transpose=True, start=True, stop=False,
                    )
                    nc.tensor.matmul(
                        out=c_ps[:, j, feats], lhsT=fc[:, half, nodes], rhs=ident_f32[:],
                        is_transpose=True, start=False, stop=True,
                    )
                    nc.tensor.transpose(o_ps[:, j, feats], o_sb[:, half, nodes], ident_f32[:])
            back_banks[g] = (c_ps, o_ps)

        def finish_c(g):
            c_ps, o_ps = back_banks[g]
            out_sb = stores.tile([P, WIDTHS[g], 2 * H], F32)
            tanh_c = work.tile([P, WIDTHS[g], H], F32)
            nc.scalar.activation(out=tanh_c[:], in_=c_ps[:], func=ACT.Tanh)
            if g < V_COPIES:
                nc.scalar.copy(out=out_sb[:, :, H : 2 * H], in_=c_ps[:])
            else:
                nc.vector.tensor_copy(out=out_sb[:, :, H : 2 * H], in_=c_ps[:])
            out_tiles[g] = (out_sb, tanh_c)

        def finish_h(g):
            c_ps, o_ps = back_banks[g]
            out_sb, tanh_c = out_tiles[g]
            nc.vector.tensor_tensor(out=out_sb[:, :, 0:H], in0=o_ps[:], in1=tanh_c[:], op=ALU.mult)
            nc.sync.dma_start(out=nodes_of(g, out).rearrange("(p l) f -> p l f", l=WIDTHS[g]), in_=out_sb[:])

        def live(g):
            return 0 <= g < ROUNDS

        with tc.manual_schedule():
            for step in range(ROUNDS + 3):
                r1, r2, r3, r4 = step, step - 1, step - 2, step - 3
                if live(r1 + AHEAD):
                    load_h(r1 + AHEAD)
                if live(r1 + AHEAD - 1):
                    load_c(r1 + AHEAD - 1)
                if live(r1):
                    max_level(r1, 4)
                if live(r4):
                    finish_h(r4)
                if live(r3):
                    multiply_iu(r3, parts_tiles[r2 % 2][:, WIDTHS[r2] - 1, 0, PACK - 1, P - 1 : P] if live(r2) else None)
                if live(r3):
                    multiply_fc(r3)
                if live(r2):
                    transpose_hc(r2)
                if live(r2):
                    regroup_hc(r2)
                if live(r1):
                    add_pairs(r1, 0)
                if live(r1):
                    max_level(r1, 2)
                if live(r2):
                    quantise_hc(r2)
                if live(r1) and WIDTHS[r1] > 1:
                    add_pairs(r1, 1)
                if live(r3):
                    transpose_back(r3)
                if live(r3):
                    finish_c(r3)
                if live(r2):
                    sum_c(r2)
                if live(r2):
                    gates(r2)
                if live(r1):
                    max_level(r1, 1)
